import numpy as np
import ml_dtypes


def mxq(x, axis, fmt="e4m3"):
    dtype, down = {"e4m3": (ml_dtypes.float8_e4m3fn, 7), "e5m2": (ml_dtypes.float8_e5m2, 14)}[fmt]
    v = np.moveaxis(np.asarray(x, np.float32).astype(ml_dtypes.bfloat16).astype(np.float64), axis, -1)
    blocks = v.reshape(v.shape[:-1] + (-1, 32))
    amax = np.abs(blocks).max(-1, keepdims=True)
    byte = np.maximum(np.where(amax > 0, np.frexp(amax)[1] - 1 + 127, 0) - down, 1)
    scale = np.exp2(byte - 127.0)
    codes = (blocks / scale).astype(np.float32).astype(dtype).astype(np.float64)
    return np.moveaxis((codes * scale).reshape(v.shape), -1, axis)


WIDE = False


def mx_kscale(k):
    if not WIDE:
        return np.ones(k)
    levels = np.array([10, -10, 5, -5, 0])
    a = np.random.permutation(np.resize(levels, k // 512 * 4)).reshape(k // 512, 4)
    idx = np.arange(k)
    return np.exp2(a[idx // 512, idx % 128 // 32])


BF16 = ml_dtypes.bfloat16


def bf(x):
    return np.asarray(x, np.float32).astype(BF16)


def f64(x):
    return np.asarray(x).astype(np.float64)


N, C, T, V, H, QK = 1, 128, 128, 256, 4, 32
K = QK * V
MQ = np.sqrt(0.5 * np.sqrt(QK))


def setup_inputs():
    s = mx_kscale(K).reshape(QK, 1, V)
    q = MQ * np.random.standard_normal((N, H, QK, T, 1)) + 1.6 * np.random.standard_normal((N, H, QK, T, V))
    k = MQ * np.random.standard_normal((N, H, QK, T, 1)) + 1.6 * np.random.standard_normal((N, H, QK, T, V))
    return {"q": bf(q * s), "k": bf(k / s),
            "alphas": bf(0.2 * (1.0 + 0.3 * np.random.standard_normal((1, H, 1, 1)))),
            "att1s": bf(np.eye(T)[None, None] + 0.05 * np.random.standard_normal((1, H, T, T)))}


def reference(q, k, alphas, att1s):
    qf = np.swapaxes(f64(q), 2, 3).reshape(N, H, T, K)
    kf = np.swapaxes(f64(k), 2, 3).reshape(N, H, T, K)
    sc = mxq(qf, 3, "e4m3") @ np.swapaxes(mxq(kf, 3, "e4m3"), 2, 3)
    return np.tanh(sc / (QK * V)) * f64(alphas) + f64(att1s)

@@ -1,0 +1,165 @@
+from contextlib import ExitStack
+
+import concourse.mybir as mybir
+from concourse.masks import make_identity
+
+F32 = mybir.dt.float32
+BF16 = mybir.dt.bfloat16
+U32 = mybir.dt.uint32
+U8 = mybir.dt.uint8
+FP8X4 = mybir.dt.float8_e4m3fn_x4
+
+P = 128
+HEADS = 4
+CHANNELS = 32
+FRAMES = 128
+JOINTS = 256
+
+CHUNK_CHANNELS = 16
+CHUNKS_PER_HEAD = CHANNELS // CHUNK_CHANNELS
+FRAME_GROUPS = P // CHUNK_CHANNELS
+FRAME_OFFSETS = FRAMES // FRAME_GROUPS
+PAIR = 2
+WORDS = JOINTS // PAIR
+CHUNK_PASSES = CHUNK_CHANNELS // PAIR
+BANK_BLOCKS = 4
+CHUNK_BANKS = FRAME_OFFSETS // BANK_BLOCKS
+TRANSPOSE_BANKS = 6
+
+assert WORDS == P and FRAMES == P
+
+FLOPS = 2 * HEADS * FRAMES * FRAMES * CHANNELS * JOINTS
+
+
+def transpose_and_quantise(nc, raw, pair_columns, bank_pool, grouped_pool, codes, scales):
+    raw_words = raw[:].bitcast(F32)
+    grouped = grouped_pool.tile([P, CHUNK_PASSES * FRAMES * 2 * PAIR], BF16, align_bytes=64)
+    grouped_words = grouped[:].bitcast(F32).rearrange("p (g x) -> p g x", g=CHUNK_PASSES)
+    bank_words = BANK_BLOCKS * FRAME_GROUPS * PAIR
+    for i in range(CHUNK_BANKS):
+        bank = bank_pool.tile([P, BANK_BLOCKS, P], F32)
+        for j in range(BANK_BLOCKS):
+            b = i * BANK_BLOCKS + j
+            nc.tensor.transpose(bank[:, j, :], raw_words[:, b * WORDS : (b + 1) * WORDS], pair_columns[:])
+        from_bank = bank[:].rearrange("p j (g r) -> p g j r", g=CHUNK_PASSES)
+        to_grouped = grouped_words[:, :, i * bank_words : (i + 1) * bank_words].rearrange(
+            "p g (j r) -> p g j r", j=BANK_BLOCKS
+        )
+        if i == CHUNK_BANKS - 1:
+            nc.vector.tensor_copy(out=to_grouped, in_=from_bank)
+        else:
+            nc.scalar.copy(out=to_grouped, in_=from_bank)
+    nc.vector.quantize_mx(out=codes[:].bitcast(FP8X4), scales=scales[:], in_=grouped[:])
+
+
+def tile_model_pa_kernel(tc, q, k, alphas, att1s, out):
+    nc = tc.nc
+    rounds = [(h, c) for h in range(HEADS) for c in range(CHUNKS_PER_HEAD)]
+    with ExitStack() as ctx:
+        consts = ctx.enter_context(tc.tile_pool(name="consts", bufs=1))
+        raw_pool = ctx.enter_context(tc.tile_pool(name="raw", bufs=2 * len(rounds)))
+        grouped_pool = ctx.enter_context(tc.tile_pool(name="grouped", bufs=3))
+        mx_pool = ctx.enter_context(tc.tile_pool(name="mx", bufs=3))
+        result_pool = ctx.enter_context(tc.tile_pool(name="result", bufs=2))
+        bank_pool = ctx.enter_context(tc.psum_pool(name="banks", bufs=TRANSPOSE_BANKS))
+        score_pool = ctx.enter_context(tc.psum_pool(name="scores", bufs=1))
+
+        alpha_bf16 = consts.tile([P, HEADS], BF16)
+        nc.scalar.dma_start(
+            out=alpha_bf16[:], in_=alphas.rearrange("o h x y -> (o h x y)").partition_broadcast(P)
+        )
+        static_map = consts.tile([P, HEADS, FRAMES], BF16)
+        nc.scalar.dma_start(out=static_map[:], in_=att1s[0].rearrange("h t u -> t h u"))
+
+        raw_q = []
+        raw_k = []
+        for h, c in rounds:
+            channels = slice(c * CHUNK_CHANNELS, (c + 1) * CHUNK_CHANNELS)
+            for source, tiles in ((q, raw_q), (k, raw_k)):
+                raw = raw_pool.tile([P, FRAME_OFFSETS * JOINTS], BF16)
+                nc.sync.dma_start(
+                    out=raw[:],
+                    in_=source[0, h, channels].rearrange("c (a b) v -> (c a) (b v)", a=FRAME_GROUPS),
+                )
+                tiles.append(raw)
+
+        identity = consts.tile([P, P], F32)
+        make_identity(nc, identity[:])
+        pair_columns = consts.tile([P, P], F32)
+        nc.vector.tensor_copy(
+            out=pair_columns[:].rearrange("p (g a e) -> p g a e", a=FRAME_GROUPS, e=PAIR),
+            in_=identity[:].rearrange("p (g e a) -> p g a e", a=FRAME_GROUPS, e=PAIR),
+        )
+        true_frames = consts.tile([P, P], F32)
+        nc.vector.tensor_copy(
+            out=true_frames[:].rearrange("p (a b) -> p a b", a=FRAME_GROUPS),
+            in_=identity[:].rearrange("p (b a) -> p a b", a=FRAME_GROUPS),
+        )
+        alpha = consts.tile([P, HEADS], F32)
+        nc.vector.tensor_copy(out=alpha[:], in_=alpha_bf16[:])
+
+        def quantised(raw, name):
+            codes = mx_pool.tile([P, CHUNK_PASSES * FRAMES], U32, align_bytes=64, name=name + "_codes")
+            scales = mx_pool.tile([P, CHUNK_PASSES * FRAMES], U8, align_bytes=64, name=name + "_scales")
+            transpose_and_quantise(nc, raw, pair_columns, bank_pool, grouped_pool, codes, scales)
+            return codes, scales
+
+        def score_passes(scores, c, q_mx, k_mx):
+            q_codes, q_scales = q_mx
+            k_codes, k_scales = k_mx
+            for g in range(CHUNK_PASSES):
+                frames = slice(g * FRAMES, (g + 1) * FRAMES)
+                nc.tensor.matmul_mx(
+                    out=scores[:],
+                    lhsT=k_codes[:, frames].bitcast(FP8X4),
+                    lhsT_scale=k_scales[:, frames],
+                    rhs=q_codes[:, frames].bitcast(FP8X4),
+                    rhs_scale=q_scales[:, frames],
+                    start=(c == 0 and g == 0),
+                    stop=(c == CHUNKS_PER_HEAD - 1 and g == CHUNK_PASSES - 1),
+                )
+
+        def squash(scores):
+            squashed = result_pool.tile([P, FRAMES], F32)
+            nc.scalar.activation(
+                out=squashed[:].rearrange("p (a b) -> p a b", a=FRAME_GROUPS),
+                in_=scores[:].rearrange("p (b a) -> p a b", a=FRAME_GROUPS),
+                func=mybir.ActivationFunctionType.Tanh,
+                scale=1.0 / (CHANNELS * JOINTS),
+            )
+            return squashed
+
+        def finish(h, squashed):
+            turned = score_pool.tile([P, FRAMES], F32)
+            nc.tensor.transpose(turned[:], squashed[:], true_frames[:])
+            result = result_pool.tile([P, FRAMES], F32)
+            nc.vector.scalar_tensor_tensor(
+                out=result[:],
+                in0=turned[:],
+                scalar=alpha[:, h : h + 1],
+                in1=static_map[:, h, :],
+                op0=mybir.AluOpType.mult,
+                op1=mybir.AluOpType.add,
+            )
+            nc.sync.dma_start(out=out[0, h], in_=result[:])
+
+        score_tiles = {}
+
+        def multiply(r, q_mx, k_mx):
+            h, c = rounds[r]
+            if c == 0:
+                score_tiles[h] = score_pool.tile([P, FRAMES], F32, name="scores")
+            score_passes(score_tiles[h], c, q_mx, k_mx)
+            if c == CHUNKS_PER_HEAD - 1:
+                return squash(score_tiles[h])
+            return None
+
+        previous = None
+        for r in range(len(rounds)):
+            q_mx = quantised(raw_q[r], "q")
+            squashed = multiply(*previous) if previous else None
+            k_mx = quantised(raw_k[r], "k")
+            if squashed is not None:
+                finish(rounds[r - 1][0], squashed)
+            previous = (r, q_mx, k_mx)
+        finish(HEADS - 1, multiply(*previous))

@@ -25,6 +25,10 @@ CHUNK_PASSES = CHUNK_CHANNELS // PAIR
 BANK_BLOCKS = 4
 CHUNK_BANKS = FRAME_OFFSETS // BANK_BLOCKS
 TRANSPOSE_BANKS = 6
+CHUNK_COLUMNS = CHUNK_PASSES * FRAMES
+BURST_PASSES = 4
+BURSTS = CHUNK_PASSES // BURST_PASSES
+MOVING_COLUMNS = 256
 
 assert WORDS == P and FRAMES == P
 
@@ -49,13 +53,20 @@ def transpose_and_quantise(nc, raw, pair_columns, bank_pool, grouped_pool, codes
             nc.vector.tensor_copy(out=to_grouped, in_=from_bank)
         else:
             nc.scalar.copy(out=to_grouped, in_=from_bank)
-    nc.vector.quantize_mx(out=codes[:].bitcast(FP8X4), scales=scales[:], in_=grouped[:])
+    burst_columns = BURST_PASSES * FRAMES
+    for n in range(BURSTS):
+        columns = slice(n * burst_columns, (n + 1) * burst_columns)
+        values = slice(n * burst_columns * 2 * PAIR, (n + 1) * burst_columns * 2 * PAIR)
+        nc.vector.quantize_mx(
+            out=codes[:, columns].bitcast(FP8X4), scales=scales[:, columns], in_=grouped[:, values]
+        )
 
 
 def tile_model_pa_kernel(tc, q, k, alphas, att1s, out):
     nc = tc.nc
     rounds = [(h, c) for h in range(HEADS) for c in range(CHUNKS_PER_HEAD)]
     with ExitStack() as ctx:
+        ctx.enter_context(tc.manual_schedule())
         consts = ctx.enter_context(tc.tile_pool(name="consts", bufs=1))
         raw_pool = ctx.enter_context(tc.tile_pool(name="raw", bufs=2 * len(rounds)))
         grouped_pool = ctx.enter_context(tc.tile_pool(name="grouped", bufs=3))
@@ -98,23 +109,27 @@ def tile_model_pa_kernel(tc, q, k, alphas, att1s, out):
         alpha = consts.tile([P, HEADS], F32)
         nc.vector.tensor_copy(out=alpha[:], in_=alpha_bf16[:])
 
-        def quantised(raw, name):
-            codes = mx_pool.tile([P, CHUNK_PASSES * FRAMES], U32, align_bytes=64, name=name + "_codes")
-            scales = mx_pool.tile([P, CHUNK_PASSES * FRAMES], U8, align_bytes=64, name=name + "_scales")
-            transpose_and_quantise(nc, raw, pair_columns, bank_pool, grouped_pool, codes, scales)
-            return codes, scales
+        table_warmer = consts.tile([P, 1], F32)
+        nc.scalar.activation(out=table_warmer[:], in_=identity[:, 0:1], func=mybir.ActivationFunctionType.Tanh)
 
-        def score_passes(scores, c, q_mx, k_mx):
-            q_codes, q_scales = q_mx
-            k_codes, k_scales = k_mx
-            for g in range(CHUNK_PASSES):
-                frames = slice(g * FRAMES, (g + 1) * FRAMES)
+        q_columns = slice(0, CHUNK_COLUMNS)
+        k_columns = slice(CHUNK_COLUMNS, 2 * CHUNK_COLUMNS)
+
+        def quantised(raw, codes, scales, columns):
+            transpose_and_quantise(
+                nc, raw, pair_columns, bank_pool, grouped_pool, codes[:, columns], scales[:, columns]
+            )
+
+        def score_passes(scores, c, n, codes, scales):
+            for g in range(n * BURST_PASSES, (n + 1) * BURST_PASSES):
+                of_q = slice(g * FRAMES, g * FRAMES + MOVING_COLUMNS)
+                of_k = slice(CHUNK_COLUMNS + g * FRAMES, CHUNK_COLUMNS + (g + 1) * FRAMES)
                 nc.tensor.matmul_mx(
                     out=scores[:],
-                    lhsT=k_codes[:, frames].bitcast(FP8X4),
-                    lhsT_scale=k_scales[:, frames],
-                    rhs=q_codes[:, frames].bitcast(FP8X4),
-                    rhs_scale=q_scales[:, frames],
+                    lhsT=codes[:, of_k].bitcast(FP8X4),
+                    lhsT_scale=scales[:, of_k],
+                    rhs=codes[:, of_q].bitcast(FP8X4),
+                    rhs_scale=scales[:, of_q],
                     start=(c == 0 and g == 0),
                     stop=(c == CHUNKS_PER_HEAD - 1 and g == CHUNK_PASSES - 1),
                 )
@@ -123,7 +138,7 @@ def tile_model_pa_kernel(tc, q, k, alphas, att1s, out):
             squashed = result_pool.tile([P, FRAMES], F32)
             nc.scalar.activation(
                 out=squashed[:].rearrange("p (a b) -> p a b", a=FRAME_GROUPS),
-                in_=scores[:].rearrange("p (b a) -> p a b", a=FRAME_GROUPS),
+                in_=scores[:, 0:FRAMES].rearrange("p (b a) -> p a b", a=FRAME_GROUPS),
                 func=mybir.ActivationFunctionType.Tanh,
                 scale=1.0 / (CHANNELS * JOINTS),
             )
@@ -143,23 +158,27 @@ def tile_model_pa_kernel(tc, q, k, alphas, att1s, out):
             )
             nc.sync.dma_start(out=out[0, h], in_=result[:])
 
-        score_tiles = {}
-
-        def multiply(r, q_mx, k_mx):
-            h, c = rounds[r]
-            if c == 0:
-                score_tiles[h] = score_pool.tile([P, FRAMES], F32, name="scores")
-            score_passes(score_tiles[h], c, q_mx, k_mx)
-            if c == CHUNKS_PER_HEAD - 1:
-                return squash(score_tiles[h])
-            return None
-
-        previous = None
-        for r in range(len(rounds)):
-            q_mx = quantised(raw_q[r], "q")
-            squashed = multiply(*previous) if previous else None
-            k_mx = quantised(raw_k[r], "k")
-            if squashed is not None:
-                finish(rounds[r - 1][0], squashed)
-            previous = (r, q_mx, k_mx)
-        finish(HEADS - 1, multiply(*previous))
+        mx_tiles = {}
+        scores = None
+        unfinished = None
+        for r in range(len(rounds) + 1):
+            if r < len(rounds):
+                codes = mx_pool.tile([P, 2 * CHUNK_COLUMNS], U32, align_bytes=64)
+                scales = mx_pool.tile([P, 2 * CHUNK_COLUMNS], U8, align_bytes=64)
+                mx_tiles[r] = (codes, scales)
+                quantised(raw_q[r], codes, scales, q_columns)
+            if unfinished:
+                finish(*unfinished)
+                unfinished = None
+            if r > 0:
+                h, c = rounds[r - 1]
+                if c == 0:
+                    scores = score_pool.tile([P, MOVING_COLUMNS], F32)
+                score_passes(scores, c, 0, *mx_tiles[r - 1])
+            if r < len(rounds):
+                quantised(raw_k[r], codes, scales, k_columns)
+            if r > 0:
+                score_passes(scores, c, 1, *mx_tiles[r - 1])
+                if c == CHUNKS_PER_HEAD - 1:
+                    unfinished = (h, squash(scores))
+        finish(*unfinished)

@@ -28,7 +28,7 @@ TRANSPOSE_BANKS = 6
 CHUNK_COLUMNS = CHUNK_PASSES * FRAMES
 BURST_PASSES = 4
 BURSTS = CHUNK_PASSES // BURST_PASSES
-MOVING_COLUMNS = 256
+MOVING_COLUMNS = FRAMES
 
 assert WORDS == P and FRAMES == P
 

@@ -24,11 +24,11 @@ WORDS = JOINTS // PAIR
 CHUNK_PASSES = CHUNK_CHANNELS // PAIR
 BANK_BLOCKS = 4
 CHUNK_BANKS = FRAME_OFFSETS // BANK_BLOCKS
-TRANSPOSE_BANKS = 6
+TRANSPOSE_BANKS = 7
 CHUNK_COLUMNS = CHUNK_PASSES * FRAMES
 BURST_PASSES = 4
 BURSTS = CHUNK_PASSES // BURST_PASSES
-MOVING_COLUMNS = FRAMES
+MOVING_COLUMNS = 256
 
 assert WORDS == P and FRAMES == P
 
@@ -38,17 +38,18 @@ FLOPS = 2 * HEADS * FRAMES * FRAMES * CHANNELS * JOINTS
 def transpose_and_quantise(nc, raw, pair_columns, bank_pool, grouped_pool, codes, scales):
     raw_words = raw[:].bitcast(F32)
     grouped = grouped_pool.tile([P, CHUNK_PASSES * FRAMES * 2 * PAIR], BF16, align_bytes=64)
-    grouped_words = grouped[:].bitcast(F32).rearrange("p (g x) -> p g x", g=CHUNK_PASSES)
-    bank_words = BANK_BLOCKS * FRAME_GROUPS * PAIR
+    grouped_words = grouped[:].bitcast(F32).rearrange(
+        "p (g a b e) -> p g a (b e)", g=CHUNK_PASSES, a=FRAME_GROUPS, e=PAIR
+    )
+    run = BANK_BLOCKS * PAIR
     for i in range(CHUNK_BANKS):
-        bank = bank_pool.tile([P, BANK_BLOCKS, P], F32)
+        bank = bank_pool.tile([P, CHUNK_PASSES * FRAME_GROUPS * run], F32)
+        blocks = bank[:].rearrange("p (n j e) -> p j n e", j=BANK_BLOCKS, e=PAIR)
         for j in range(BANK_BLOCKS):
             b = i * BANK_BLOCKS + j
-            nc.tensor.transpose(bank[:, j, :], raw_words[:, b * WORDS : (b + 1) * WORDS], pair_columns[:])
-        from_bank = bank[:].rearrange("p j (g r) -> p g j r", g=CHUNK_PASSES)
-        to_grouped = grouped_words[:, :, i * bank_words : (i + 1) * bank_words].rearrange(
-            "p g (j r) -> p g j r", j=BANK_BLOCKS
-        )
+            nc.tensor.transpose(blocks[:, j], raw_words[:, b * WORDS : (b + 1) * WORDS], pair_columns[:])
+        from_bank = bank[:].rearrange("p (g a x) -> p g a x", g=CHUNK_PASSES, a=FRAME_GROUPS)
+        to_grouped = grouped_words[:, :, :, i * run : (i + 1) * run]
         if i == CHUNK_BANKS - 1:
             nc.vector.tensor_copy(out=to_grouped, in_=from_bank)
         else:
@@ -71,28 +72,29 @@ def tile_model_pa_kernel(tc, q, k, alphas, att1s, out):
         raw_pool = ctx.enter_context(tc.tile_pool(name="raw", bufs=2 * len(rounds)))
         grouped_pool = ctx.enter_context(tc.tile_pool(name="grouped", bufs=3))
         mx_pool = ctx.enter_context(tc.tile_pool(name="mx", bufs=3))
-        result_pool = ctx.enter_context(tc.tile_pool(name="result", bufs=2))
+        result_pool = ctx.enter_context(tc.tile_pool(name="result", bufs=HEADS))
         bank_pool = ctx.enter_context(tc.psum_pool(name="banks", bufs=TRANSPOSE_BANKS))
         score_pool = ctx.enter_context(tc.psum_pool(name="scores", bufs=1))
 
+        raw_k = []
+        raw_q = []
+        for h, c in rounds:
+            channels = slice(c * CHUNK_CHANNELS, (c + 1) * CHUNK_CHANNELS)
+            for source, tiles in ((k, raw_k), (q, raw_q)):
+                raw = raw_pool.tile([P, FRAME_OFFSETS * JOINTS], BF16)
+                rows = source[0, h, channels].rearrange("c (a b) v -> (c a) (b v)", a=FRAME_GROUPS)
+                pieces = CHUNK_BANKS if (h, c) == rounds[-1] and source is q else 1
+                width = FRAME_OFFSETS * JOINTS // pieces
+                for n in range(pieces):
+                    part = slice(n * width, (n + 1) * width)
+                    nc.sync.dma_start(out=raw[:, part], in_=rows[:, part])
+                tiles.append(raw)
         alpha_bf16 = consts.tile([P, HEADS], BF16)
-        nc.scalar.dma_start(
+        nc.sync.dma_start(
             out=alpha_bf16[:], in_=alphas.rearrange("o h x y -> (o h x y)").partition_broadcast(P)
         )
         static_map = consts.tile([P, HEADS, FRAMES], BF16)
-        nc.scalar.dma_start(out=static_map[:], in_=att1s[0].rearrange("h t u -> t h u"))
-
-        raw_q = []
-        raw_k = []
-        for h, c in rounds:
-            channels = slice(c * CHUNK_CHANNELS, (c + 1) * CHUNK_CHANNELS)
-            for source, tiles in ((q, raw_q), (k, raw_k)):
-                raw = raw_pool.tile([P, FRAME_OFFSETS * JOINTS], BF16)
-                nc.sync.dma_start(
-                    out=raw[:],
-                    in_=source[0, h, channels].rearrange("c (a b) v -> (c a) (b v)", a=FRAME_GROUPS),
-                )
-                tiles.append(raw)
+        nc.sync.dma_start(out=static_map[:], in_=att1s[0].rearrange("h t u -> t h u"))
 
         identity = consts.tile([P, P], F32)
         make_identity(nc, identity[:])
@@ -101,19 +103,11 @@ def tile_model_pa_kernel(tc, q, k, alphas, att1s, out):
             out=pair_columns[:].rearrange("p (g a e) -> p g a e", a=FRAME_GROUPS, e=PAIR),
             in_=identity[:].rearrange("p (g e a) -> p g a e", a=FRAME_GROUPS, e=PAIR),
         )
-        true_frames = consts.tile([P, P], F32)
-        nc.vector.tensor_copy(
-            out=true_frames[:].rearrange("p (a b) -> p a b", a=FRAME_GROUPS),
-            in_=identity[:].rearrange("p (b a) -> p a b", a=FRAME_GROUPS),
-        )
-        alpha = consts.tile([P, HEADS], F32)
-        nc.vector.tensor_copy(out=alpha[:], in_=alpha_bf16[:])
-
         table_warmer = consts.tile([P, 1], F32)
         nc.scalar.activation(out=table_warmer[:], in_=identity[:, 0:1], func=mybir.ActivationFunctionType.Tanh)
 
-        q_columns = slice(0, CHUNK_COLUMNS)
-        k_columns = slice(CHUNK_COLUMNS, 2 * CHUNK_COLUMNS)
+        k_columns = slice(0, CHUNK_COLUMNS)
+        q_columns = slice(CHUNK_COLUMNS, 2 * CHUNK_COLUMNS)
 
         def quantised(raw, codes, scales, columns):
             transpose_and_quantise(
@@ -122,63 +116,56 @@ def tile_model_pa_kernel(tc, q, k, alphas, att1s, out):
 
         def score_passes(scores, c, n, codes, scales):
             for g in range(n * BURST_PASSES, (n + 1) * BURST_PASSES):
-                of_q = slice(g * FRAMES, g * FRAMES + MOVING_COLUMNS)
-                of_k = slice(CHUNK_COLUMNS + g * FRAMES, CHUNK_COLUMNS + (g + 1) * FRAMES)
+                of_k = slice(g * FRAMES, g * FRAMES + MOVING_COLUMNS)
+                of_q = slice(CHUNK_COLUMNS + g * FRAMES, CHUNK_COLUMNS + (g + 1) * FRAMES)
                 nc.tensor.matmul_mx(
                     out=scores[:],
-                    lhsT=codes[:, of_k].bitcast(FP8X4),
-                    lhsT_scale=scales[:, of_k],
-                    rhs=codes[:, of_q].bitcast(FP8X4),
-                    rhs_scale=scales[:, of_q],
+                    lhsT=codes[:, of_q].bitcast(FP8X4),
+                    lhsT_scale=scales[:, of_q],
+                    rhs=codes[:, of_k].bitcast(FP8X4),
+                    rhs_scale=scales[:, of_k],
                     start=(c == 0 and g == 0),
                     stop=(c == CHUNKS_PER_HEAD - 1 and g == CHUNK_PASSES - 1),
                 )
 
-        def squash(scores):
-            squashed = result_pool.tile([P, FRAMES], F32)
-            nc.scalar.activation(
-                out=squashed[:].rearrange("p (a b) -> p a b", a=FRAME_GROUPS),
-                in_=scores[:, 0:FRAMES].rearrange("p (b a) -> p a b", a=FRAME_GROUPS),
-                func=mybir.ActivationFunctionType.Tanh,
-                scale=1.0 / (CHANNELS * JOINTS),
-            )
-            return squashed
-
-        def finish(h, squashed):
-            turned = score_pool.tile([P, FRAMES], F32)
-            nc.tensor.transpose(turned[:], squashed[:], true_frames[:])
-            result = result_pool.tile([P, FRAMES], F32)
-            nc.vector.scalar_tensor_tensor(
-                out=result[:],
-                in0=turned[:],
-                scalar=alpha[:, h : h + 1],
-                in1=static_map[:, h, :],
-                op0=mybir.AluOpType.mult,
-                op1=mybir.AluOpType.add,
-            )
-            nc.sync.dma_start(out=out[0, h], in_=result[:])
-
         mx_tiles = {}
         scores = None
-        unfinished = None
+        squashed = []
         for r in range(len(rounds) + 1):
             if r < len(rounds):
                 codes = mx_pool.tile([P, 2 * CHUNK_COLUMNS], U32, align_bytes=64)
                 scales = mx_pool.tile([P, 2 * CHUNK_COLUMNS], U8, align_bytes=64)
                 mx_tiles[r] = (codes, scales)
-                quantised(raw_q[r], codes, scales, q_columns)
-            if unfinished:
-                finish(*unfinished)
-                unfinished = None
+                quantised(raw_k[r], codes, scales, k_columns)
             if r > 0:
                 h, c = rounds[r - 1]
                 if c == 0:
                     scores = score_pool.tile([P, MOVING_COLUMNS], F32)
                 score_passes(scores, c, 0, *mx_tiles[r - 1])
             if r < len(rounds):
-                quantised(raw_k[r], codes, scales, k_columns)
+                quantised(raw_q[r], codes, scales, q_columns)
             if r > 0:
                 score_passes(scores, c, 1, *mx_tiles[r - 1])
                 if c == CHUNKS_PER_HEAD - 1:
-                    unfinished = (h, squash(scores))
-        finish(*unfinished)
+                    squashed_h = result_pool.tile([P, FRAMES], F32)
+                    nc.scalar.activation(
+                        out=squashed_h[:],
+                        in_=scores[:, 0:FRAMES],
+                        func=mybir.ActivationFunctionType.Tanh,
+                        scale=1.0 / (CHANNELS * JOINTS),
+                    )
+                    squashed.append(squashed_h)
+
+        alpha = consts.tile([P, HEADS], F32)
+        nc.vector.tensor_copy(out=alpha[:], in_=alpha_bf16[:])
+        for h in range(HEADS):
+            result = result_pool.tile([P, FRAMES], F32)
+            nc.vector.scalar_tensor_tensor(
+                out=result[:],
+                in0=squashed[h][:],
+                scalar=alpha[:, h : h + 1],
+                in1=static_map[:, h, :],
+                op0=mybir.AluOpType.mult,
+                op1=mybir.AluOpType.add,
+            )
+            nc.sync.dma_start(out=out[0, h], in_=result[:])

from contextlib import ExitStack

import concourse.mybir as mybir
from concourse.masks import make_identity

F32 = mybir.dt.float32
BF16 = mybir.dt.bfloat16
U32 = mybir.dt.uint32
U8 = mybir.dt.uint8
FP8X4 = mybir.dt.float8_e4m3fn_x4

P = 128
HEADS = 4
CHANNELS = 32
FRAMES = 128
JOINTS = 256

CHUNK_CHANNELS = 16
CHUNKS_PER_HEAD = CHANNELS // CHUNK_CHANNELS
FRAME_GROUPS = P // CHUNK_CHANNELS
FRAME_OFFSETS = FRAMES // FRAME_GROUPS
PAIR = 2
WORDS = JOINTS // PAIR
CHUNK_PASSES = CHUNK_CHANNELS // PAIR
BANK_BLOCKS = 4
CHUNK_BANKS = FRAME_OFFSETS // BANK_BLOCKS
TRANSPOSE_BANKS = 7
CHUNK_COLUMNS = CHUNK_PASSES * FRAMES
BURST_PASSES = 4
BURSTS = CHUNK_PASSES // BURST_PASSES
MOVING_COLUMNS = 256

assert WORDS == P and FRAMES == P

FLOPS = 2 * HEADS * FRAMES * FRAMES * CHANNELS * JOINTS


def transpose_and_quantise(nc, raw, pair_columns, bank_pool, grouped_pool, codes, scales):
    raw_words = raw[:].bitcast(F32)
    grouped = grouped_pool.tile([P, CHUNK_PASSES * FRAMES * 2 * PAIR], BF16, align_bytes=64)
    grouped_words = grouped[:].bitcast(F32).rearrange(
        "p (g a b e) -> p g a (b e)", g=CHUNK_PASSES, a=FRAME_GROUPS, e=PAIR
    )
    run = BANK_BLOCKS * PAIR
    for i in range(CHUNK_BANKS):
        bank = bank_pool.tile([P, CHUNK_PASSES * FRAME_GROUPS * run], F32)
        blocks = bank[:].rearrange("p (n j e) -> p j n e", j=BANK_BLOCKS, e=PAIR)
        for j in range(BANK_BLOCKS):
            b = i * BANK_BLOCKS + j
            nc.tensor.transpose(blocks[:, j], raw_words[:, b * WORDS : (b + 1) * WORDS], pair_columns[:])
        from_bank = bank[:].rearrange("p (g a x) -> p g a x", g=CHUNK_PASSES, a=FRAME_GROUPS)
        to_grouped = grouped_words[:, :, :, i * run : (i + 1) * run]
        if i == CHUNK_BANKS - 1:
            nc.vector.tensor_copy(out=to_grouped, in_=from_bank)
        else:
            nc.scalar.copy(out=to_grouped, in_=from_bank)
    burst_columns = BURST_PASSES * FRAMES
    for n in range(BURSTS):
        columns = slice(n * burst_columns, (n + 1) * burst_columns)
        values = slice(n * burst_columns * 2 * PAIR, (n + 1) * burst_columns * 2 * PAIR)
        nc.vector.quantize_mx(
            out=codes[:, columns].bitcast(FP8X4), scales=scales[:, columns], in_=grouped[:, values]
        )


def tile_model_pa_kernel(tc, q, k, alphas, att1s, out):
    nc = tc.nc
    rounds = [(h, c) for h in range(HEADS) for c in range(CHUNKS_PER_HEAD)]
    with ExitStack() as ctx:
        ctx.enter_context(tc.manual_schedule())
        consts = ctx.enter_context(tc.tile_pool(name="consts", bufs=1))
        raw_pool = ctx.enter_context(tc.tile_pool(name="raw", bufs=2 * len(rounds)))
        grouped_pool = ctx.enter_context(tc.tile_pool(name="grouped", bufs=3))
        mx_pool = ctx.enter_context(tc.tile_pool(name="mx", bufs=3))
        result_pool = ctx.enter_context(tc.tile_pool(name="result", bufs=HEADS))
        bank_pool = ctx.enter_context(tc.psum_pool(name="banks", bufs=TRANSPOSE_BANKS))
        score_pool = ctx.enter_context(tc.psum_pool(name="scores", bufs=1))

        raw_k = []
        raw_q = []
        for h, c in rounds:
            channels = slice(c * CHUNK_CHANNELS, (c + 1) * CHUNK_CHANNELS)
            for source, tiles in ((k, raw_k), (q, raw_q)):
                raw = raw_pool.tile([P, FRAME_OFFSETS * JOINTS], BF16)
                rows = source[0, h, channels].rearrange("c (a b) v -> (c a) (b v)", a=FRAME_GROUPS)
                pieces = CHUNK_BANKS if (h, c) == rounds[-1] and source is q else 1
                width = FRAME_OFFSETS * JOINTS // pieces
                for n in range(pieces):
                    part = slice(n * width, (n + 1) * width)
                    nc.sync.dma_start(out=raw[:, part], in_=rows[:, part])
                tiles.append(raw)
        alpha_bf16 = consts.tile([P, HEADS], BF16)
        nc.sync.dma_start(
            out=alpha_bf16[:], in_=alphas.rearrange("o h x y -> (o h x y)").partition_broadcast(P)
        )
        static_map = consts.tile([P, HEADS, FRAMES], BF16)
        nc.sync.dma_start(out=static_map[:], in_=att1s[0].rearrange("h t u -> t h u"))

        identity = consts.tile([P, P], F32)
        make_identity(nc, identity[:])
        pair_columns = consts.tile([P, P], F32)
        nc.vector.tensor_copy(
            out=pair_columns[:].rearrange("p (g a e) -> p g a e", a=FRAME_GROUPS, e=PAIR),
            in_=identity[:].rearrange("p (g e a) -> p g a e", a=FRAME_GROUPS, e=PAIR),
        )
        table_warmer = consts.tile([P, 1], F32)
        nc.scalar.activation(out=table_warmer[:], in_=identity[:, 0:1], func=mybir.ActivationFunctionType.Tanh)

        k_columns = slice(0, CHUNK_COLUMNS)
        q_columns = slice(CHUNK_COLUMNS, 2 * CHUNK_COLUMNS)

        def quantised(raw, codes, scales, columns):
            transpose_and_quantise(
                nc, raw, pair_columns, bank_pool, grouped_pool, codes[:, columns], scales[:, columns]
            )

        def score_passes(scores, c, n, codes, scales):
            for g in range(n * BURST_PASSES, (n + 1) * BURST_PASSES):
                of_k = slice(g * FRAMES, g * FRAMES + MOVING_COLUMNS)
                of_q = slice(CHUNK_COLUMNS + g * FRAMES, CHUNK_COLUMNS + (g + 1) * FRAMES)
                nc.tensor.matmul_mx(
                    out=scores[:],
                    lhsT=codes[:, of_q].bitcast(FP8X4),
                    lhsT_scale=scales[:, of_q],
                    rhs=codes[:, of_k].bitcast(FP8X4),
                    rhs_scale=scales[:, of_k],
                    start=(c == 0 and g == 0),
                    stop=(c == CHUNKS_PER_HEAD - 1 and g == CHUNK_PASSES - 1),
                )

        mx_tiles = {}
        scores = None
        squashed = []
        for r in range(len(rounds) + 1):
            if r < len(rounds):
                codes = mx_pool.tile([P, 2 * CHUNK_COLUMNS], U32, align_bytes=64)
                scales = mx_pool.tile([P, 2 * CHUNK_COLUMNS], U8, align_bytes=64)
                mx_tiles[r] = (codes, scales)
                quantised(raw_k[r], codes, scales, k_columns)
            if r > 0:
                h, c = rounds[r - 1]
                if c == 0:
                    scores = score_pool.tile([P, MOVING_COLUMNS], F32)
                score_passes(scores, c, 0, *mx_tiles[r - 1])
            if r < len(rounds):
                quantised(raw_q[r], codes, scales, q_columns)
            if r > 0:
                score_passes(scores, c, 1, *mx_tiles[r - 1])
                if c == CHUNKS_PER_HEAD - 1:
                    squashed_h = result_pool.tile([P, FRAMES], F32)
                    nc.scalar.activation(
                        out=squashed_h[:],
                        in_=scores[:, 0:FRAMES],
                        func=mybir.ActivationFunctionType.Tanh,
                        scale=1.0 / (CHANNELS * JOINTS),
                    )
                    squashed.append(squashed_h)

        alpha = consts.tile([P, HEADS], F32)
        nc.vector.tensor_copy(out=alpha[:], in_=alpha_bf16[:])
        for h in range(HEADS):
            result = result_pool.tile([P, FRAMES], F32)
            nc.vector.scalar_tensor_tensor(
                out=result[:],
                in0=squashed[h][:],
                scalar=alpha[:, h : h + 1],
                in1=static_map[:, h, :],
                op0=mybir.AluOpType.mult,
                op1=mybir.AluOpType.add,
            )
            nc.sync.dma_start(out=out[0, h], in_=result[:])
